import numpy as np
import ml_dtypes


def mxq(x, axis, fmt="e4m3"):
    dtype, down = {"e4m3": (ml_dtypes.float8_e4m3fn, 7), "e5m2": (ml_dtypes.float8_e5m2, 14)}[fmt]
    v = np.moveaxis(np.asarray(x, np.float32).astype(ml_dtypes.bfloat16).astype(np.float64), axis, -1)
    blocks = v.reshape(v.shape[:-1] + (-1, 32))
    amax = np.abs(blocks).max(-1, keepdims=True)
    byte = np.maximum(np.where(amax > 0, np.frexp(amax)[1] - 1 + 127, 0) - down, 1)
    scale = np.exp2(byte - 127.0)
    codes = (blocks / scale).astype(np.float32).astype(dtype).astype(np.float64)
    return np.moveaxis((codes * scale).reshape(v.shape), -1, axis)


WIDE = False


def mx_kscale(k):
    if not WIDE:
        return np.ones(k)
    levels = np.array([10, -10, 5, -5, 0])
    a = np.random.permutation(np.resize(levels, k // 512 * 4)).reshape(k // 512, 4)
    idx = np.arange(k)
    return np.exp2(a[idx // 512, idx % 128 // 32])


BF16 = ml_dtypes.bfloat16


def bf(x):
    return np.asarray(x, np.float32).astype(BF16)


def f64(x):
    return np.asarray(x).astype(np.float64)


E2M1 = np.array([0.0, 0.5, 1.0, 1.5, 2.0, 3.0, 4.0, 6.0, -0.0, -0.5, -1.0, -1.5, -2.0, -3.0, -4.0, -6.0])


def pack_weight(w, fmt):
    k, n = w.shape
    w = f64(bf(w)).reshape(k // 32, 32, n)
    amax = np.abs(w).max(1)
    if fmt == "e4m3":
        byte = np.frexp(amax)[1] - 1 + 127 - 7
    else:
        mant, ex = np.frexp(amax / 6.0)
        byte = np.where(mant > 0.5, ex, ex - 1) + 127
    byte = np.clip(np.where(amax > 0, byte, 1), 1, 254)
    scaled = (w * np.exp2(127.0 - byte)[:, None, :]).reshape(k, n).astype(np.float32)
    by_word = np.ascontiguousarray(scaled.reshape(k // 512, 128, 4, n).transpose(0, 1, 3, 2))
    if fmt == "e4m3":
        words = by_word.astype(ml_dtypes.float8_e4m3fn).view(np.uint8)
    else:
        c = by_word.astype(ml_dtypes.float4_e2m1fn).view(np.uint8) & 0xF
        words = c[..., 0::2] | (c[..., 1::2] << 4)
    return np.ascontiguousarray(words), np.ascontiguousarray(byte.astype(np.uint8).reshape(k // 512, 16, n))


def unpack_weight(words, scales, fmt):
    g, p, n, _ = words.shape
    if fmt == "e4m3":
        vals = np.ascontiguousarray(words).view(ml_dtypes.float8_e4m3fn).astype(np.float64)
    else:
        nib = np.empty((g, p, n, 4), np.uint8)
        nib[..., 0::2] = words & 0xF
        nib[..., 1::2] = words >> 4
        vals = E2M1[nib]
    vals = vals * np.repeat(np.exp2(scales.astype(np.float64) - 127.0), 8, axis=1)[..., None]
    return vals.transpose(0, 1, 3, 2).reshape(g * 512, n)

def pack4(w):
    words, scales = pack_weight(w, "e2m1")
    return words.reshape(words.shape[0], 128, -1), scales


def unpack4(words, scales):
    return unpack_weight(words.reshape(words.shape[0], 128, -1, 2), scales, "e2m1")


B, IN, H, G, GA, GB = 1024, 1024, 1024, 6, 4, 2
EPS = 1e-5


def layer_norm(v, g, b):
    mu = v.mean(-1, keepdims=True)
    var = np.square(v - mu).mean(-1, keepdims=True)
    return (v - mu) / np.sqrt(var + EPS) * g + b


def sigmoid(v):
    return 1.0 / (1.0 + np.exp(-v))


def setup_inputs():
    s = mx_kscale(IN)
    x = bf(np.random.standard_normal((B, IN)) * s)
    h = bf(np.random.standard_normal((B, H)))
    c = bf(np.tanh(1.4 * np.random.standard_normal((B, H))))
    W_u_words, W_u_scales = pack4((np.random.standard_normal((H, H)) / np.sqrt(H)).T)
    U_u_words, U_u_scales = pack4((np.random.standard_normal((H, IN)) / np.sqrt(IN) / s).T)
    ln_gamma = bf(1.0 + 0.1 * np.random.standard_normal((GB, H)))
    ln_beta = bf(0.2 * np.random.standard_normal((GB, H)))
    return {"x": x,
            "h": h,
            "c": c,
            "W_u_words": W_u_words,
            "W_u_scales": W_u_scales,
            "U_u_words": U_u_words,
            "U_u_scales": U_u_scales,
            "ln_gamma": ln_gamma,
            "ln_beta": ln_beta}


def reference(x, h, c, W_u_words, W_u_scales, U_u_words, U_u_scales, ln_gamma, ln_beta):
    g_uh, g_ux = f64(ln_gamma)
    b_uh, b_ux = f64(ln_beta)
    hf = f64(h)
    u = sigmoid(layer_norm(mxq(hf, 1, "e4m3") @ unpack4(W_u_words, W_u_scales), g_uh, b_uh)
                + layer_norm(mxq(f64(x), 1, "e4m3") @ unpack4(U_u_words, U_u_scales), g_ux, b_ux))
    return (1.0 - u) * hf + u * f64(c)

@@ -1,0 +1,292 @@
+import concourse.mybir as mybir
+from concourse.masks import make_identity
+
+F32 = mybir.dt.float32
+BF16 = mybir.dt.bfloat16
+I32 = mybir.dt.int32
+U32 = mybir.dt.uint32
+U8 = mybir.dt.uint8
+FP8X4 = mybir.dt.float8_e4m3fn_x4
+FP4X4 = mybir.dt.float4_e2m1fn_x4
+ACT = mybir.ActivationFunctionType
+ALU = mybir.AluOpType
+
+P = 128
+ROWS = 1024
+TILES = ROWS // P
+K = 1024
+N = 1024
+PACK = 4
+GROUPS = K // (P * PACK)
+GROUP_WORDS = P * PACK // 2
+BANK = 512
+HALVES = N // BANK
+EPS = 1e-5
+
+FLOPS = 2 * 2 * ROWS * K * N
+
+
+def tile_layernormgrucell_pb_kernel(
+    tc, x, h, c, W_u_words, W_u_scales, U_u_words, U_u_scales, ln_gamma, ln_beta, out
+):
+    nc = tc.nc
+    with (
+        tc.tile_pool(name="keep", bufs=1) as keep,
+        tc.tile_pool(name="operand", bufs=4) as operand,
+        tc.tile_pool(name="small", bufs=4) as small,
+        tc.tile_pool(name="work", bufs=3) as work,
+        tc.psum_pool(name="turned_banks", bufs=2) as turned_banks,
+        tc.psum_pool(name="product_banks", bufs=6) as product_banks,
+        tc.manual_schedule(),
+    ):
+        x_rows = x.rearrange("(p t) k -> p t k", t=TILES)
+        h_rows = h.rearrange("(p t) k -> p t k", t=TILES)
+        c_rows = c.rearrange("(p t) k -> p t k", t=TILES)
+        out_rows = out.rearrange("(p t) n -> p t n", t=TILES)
+        x_sb = keep.tile([P, TILES, K], BF16)
+        h_sb = keep.tile([P, TILES, K], BF16)
+        c_sb = keep.tile([P, TILES, N], BF16)
+
+        def load_weight(words, scales, words_sb, planes):
+            nc.vector.memset(planes[:].rearrange("p g n -> p (g n)").bitcast(I32), 0)
+            for quadrant in range(4):
+                nc.sync.dma_start(
+                    out=planes[32 * quadrant : 32 * quadrant + 4, :, :].bitcast(I32),
+                    in_=scales.bitcast(I32)[:, 4 * quadrant : 4 * quadrant + 4, :].rearrange(
+                        "g r n -> r g n"
+                    ),
+                )
+            nc.sync.dma_start(
+                out=words_sb[:].bitcast(I32), in_=words.bitcast(I32).rearrange("g p b -> p g b")
+            )
+
+        w_words = keep.tile([P, GROUPS, 2 * N], U8, align_bytes=64)
+        w_planes = keep.tile([P, GROUPS, N], U8, align_bytes=64)
+        u_words = keep.tile([P, GROUPS, 2 * N], U8, align_bytes=64)
+        u_planes = keep.tile([P, GROUPS, N], U8, align_bytes=64)
+        gamma_all = keep.tile([P, 2, N], BF16)
+        beta_all = keep.tile([P, 2, N], BF16)
+
+        nc.sync.dma_start(out=h_sb[:, 0, :], in_=h_rows[:, 0, :])
+        nc.sync.dma_start(out=x_sb[:, 0, :], in_=x_rows[:, 0, :])
+        load_weight(W_u_words, W_u_scales, w_words, w_planes)
+        load_weight(U_u_words, U_u_scales, u_words, u_planes)
+        nc.sync.dma_start(
+            out=gamma_all[:].rearrange("p j n -> p (j n)"),
+            in_=ln_gamma.rearrange("j n -> (j n)").partition_broadcast(P),
+        )
+        nc.sync.dma_start(
+            out=beta_all[:].rearrange("p j n -> p (j n)"),
+            in_=ln_beta.rearrange("j n -> (j n)").partition_broadcast(P),
+        )
+        nc.sync.dma_start(out=c_sb[:, 0, :], in_=c_rows[:, 0, :])
+        for t in range(1, TILES):
+            nc.sync.dma_start(out=h_sb[:, t, :], in_=h_rows[:, t, :])
+            nc.sync.dma_start(out=x_sb[:, t, :], in_=x_rows[:, t, :])
+            nc.sync.dma_start(out=c_sb[:, t, :], in_=c_rows[:, t, :])
+
+        identity = keep.tile([P, P], F32)
+        make_identity(nc, identity[:])
+        minus_half = keep.tile([P, 2], F32)
+        nc.gpsimd.memset(minus_half[:], -0.5)
+        first_table = keep.tile([P, 1], F32)
+        nc.scalar.activation(out=first_table[:], in_=minus_half[:, 0:1], func=ACT.Sigmoid)
+        beta_sum = keep.tile([P, N], F32)
+        nc.gpsimd.tensor_tensor(
+            out=beta_sum[:], in0=beta_all[:, 0, :], in1=beta_all[:, 1, :], op=ALU.add
+        )
+        diff = keep.tile([P, TILES, N], F32)
+
+        activations = (h_sb, x_sb)
+        weights = ((w_words, w_planes), (u_words, u_planes))
+        turned = {}
+        grouped = {}
+        quantised = {}
+        product = {}
+        neg_mean = {}
+        sum_sq = {}
+        rstd = {}
+        centred = {}
+        pre_gate = {}
+        gate = {}
+
+        def difference(t):
+            for half in range(HALVES):
+                cols = slice(BANK * half, BANK * (half + 1))
+                nc.gpsimd.tensor_tensor(
+                    out=diff[:, t, cols], in0=c_sb[:, t, cols], in1=h_sb[:, t, cols], op=ALU.subtract
+                )
+
+        def transpose(t):
+            for j in range(2):
+                words = activations[j][:, t, :].bitcast(F32)
+                bank = turned_banks.tile([P, GROUPS, 2, P], F32)
+                for g in range(GROUPS):
+                    for u in range(2):
+                        nc.tensor.transpose(
+                            bank[:, g, u, :],
+                            words[:, GROUP_WORDS * g + u : GROUP_WORDS * (g + 1) : 2],
+                            identity[:],
+                        )
+                turned[t, j] = bank
+
+        def regroup(t):
+            for j in range(2):
+                lined_up = operand.tile([P, GROUPS, P, PACK], BF16, align_bytes=64)
+                nc.scalar.copy(
+                    out=lined_up[:]
+                    .rearrange("p g r t -> p (g r t)")
+                    .bitcast(F32)
+                    .rearrange("p (g r u) -> p g r u", g=GROUPS, u=2),
+                    in_=turned[t, j][:].rearrange("p g u r -> p g r u"),
+                )
+                grouped[t, j] = lined_up
+
+        def quantise(t):
+            for j in range(2):
+                codes = operand.tile([P, GROUPS, P], U32, align_bytes=64)
+                plane = operand.tile([P, GROUPS, P], U8, align_bytes=64)
+                nc.vector.quantize_mx(
+                    out=codes[:].rearrange("p g r -> p (g r)").bitcast(FP8X4),
+                    scales=plane[:].rearrange("p g r -> p (g r)"),
+                    in_=grouped[t, j][:].rearrange("p g r t -> p (g r t)"),
+                )
+                quantised[t, j] = (codes, plane)
+
+        def project(t):
+            for j in range(2):
+                codes, plane = quantised[t, j]
+                words_sb, planes = weights[j]
+                for half in range(HALVES):
+                    bank = product_banks.tile([P, BANK], F32)
+                    for g in range(GROUPS):
+                        nc.tensor.matmul_mx(
+                            out=bank[:],
+                            lhsT=codes[:, g, :].bitcast(FP8X4),
+                            lhsT_scale=plane[:, g, :],
+                            rhs=words_sb[:, g, 2 * BANK * half : 2 * BANK * (half + 1)].bitcast(FP4X4),
+                            rhs_scale=planes[:, g, BANK * half : BANK * (half + 1)],
+                            start=(g == 0),
+                            stop=(g == GROUPS - 1),
+                        )
+                    product[t, j, half] = bank
+
+        def means(t):
+            parts = small.tile([P, 2, HALVES], F32)
+            minus = small.tile([P, 2], F32)
+            for j in range(2):
+                for half in range(HALVES):
+                    unused = work.tile([P, BANK], BF16)
+                    nc.scalar.activation(
+                        out=unused[:],
+                        in_=product[t, j, half][:],
+                        func=ACT.Identity,
+                        scale=-1.0 / N,
+                        accum_out=parts[:, j, half : half + 1],
+                    )
+            for j in range(2):
+                nc.scalar.activation(
+                    out=minus[:, j : j + 1],
+                    in_=parts[:, j, 0:1],
+                    func=ACT.Identity,
+                    bias=parts[:, j, 1:2],
+                    scale=1.0,
+                )
+            neg_mean[t] = minus
+            squares = small.tile([P, 2, HALVES], F32)
+            sum_sq[t] = squares
+
+        def squared_deviations(t, j):
+            for half in range(HALVES):
+                unused = work.tile([P, BANK], BF16)
+                nc.scalar.activation(
+                    out=unused[:],
+                    in_=product[t, j, half][:],
+                    func=ACT.Square,
+                    bias=neg_mean[t][:, j : j + 1],
+                    scale=1.0,
+                    accum_out=sum_sq[t][:, j, half : half + 1],
+                )
+
+        def reciprocal_deviation(t):
+            variance = small.tile([P, 2], F32)
+            inverse = small.tile([P, 2], F32)
+            nc.gpsimd.tensor_tensor(
+                out=variance[:], in0=sum_sq[t][:, :, 0], in1=sum_sq[t][:, :, 1], op=ALU.add
+            )
+            nc.gpsimd.tensor_scalar(
+                out=variance[:], in0=variance[:], scalar1=1.0 / N, scalar2=EPS, op0=ALU.mult, op1=ALU.add
+            )
+            nc.gpsimd.tensor_tensor(out=inverse[:], in0=variance[:], in1=minus_half[:], op=ALU.pow)
+            rstd[t] = inverse
+
+        def centre(t):
+            for j in range(2):
+                scaled = work.tile([P, N], F32, bufs=4)
+                for half in range(HALVES):
+                    cols = slice(BANK * half, BANK * (half + 1))
+                    nc.vector.scalar_tensor_tensor(
+                        out=scaled[:, cols],
+                        in0=product[t, j, half][:],
+                        scalar=neg_mean[t][:, j : j + 1],
+                        in1=gamma_all[:, j, cols],
+                        op0=ALU.add,
+                        op1=ALU.mult,
+                    )
+                centred[t, j] = scaled
+
+        def combine(t):
+            total = work.tile([P, N], F32)
+            nc.vector.scalar_tensor_tensor(
+                out=total[:], in0=centred[t, 0][:], scalar=rstd[t][:, 0:1], in1=beta_sum[:],
+                op0=ALU.mult, op1=ALU.add,
+            )
+            nc.vector.scalar_tensor_tensor(
+                out=total[:], in0=centred[t, 1][:], scalar=rstd[t][:, 1:2], in1=total[:],
+                op0=ALU.mult, op1=ALU.add,
+            )
+            pre_gate[t] = total
+
+        def sigmoid(t):
+            update = work.tile([P, N], F32)
+            for half in range(HALVES):
+                cols = slice(BANK * half, BANK * (half + 1))
+                nc.scalar.activation(out=update[:, cols], in_=pre_gate[t][:, cols], func=ACT.Sigmoid)
+            gate[t] = update
+
+        def blend(t):
+            result = work.tile([P, N], F32)
+            for half in range(HALVES):
+                cols = slice(BANK * half, BANK * (half + 1))
+                nc.vector.tensor_tensor(
+                    out=result[:, cols], in0=gate[t][:, cols], in1=diff[:, t, cols], op=ALU.mult
+                )
+                nc.vector.tensor_tensor(
+                    out=result[:, cols], in0=result[:, cols], in1=h_sb[:, t, cols], op=ALU.add
+                )
+                nc.sync.dma_start(out=out_rows[:, t, cols], in_=result[:, cols])
+
+        def in_range(t):
+            return 0 <= t < TILES
+
+        for t in range(-2, TILES + 1):
+            if in_range(t + 2):
+                transpose(t + 2)
+            if in_range(t + 1):
+                project(t + 1)
+            if in_range(t):
+                means(t)
+                squared_deviations(t, 0)
+                squared_deviations(t, 1)
+                reciprocal_deviation(t)
+                centre(t)
+            if in_range(t - 1):
+                sigmoid(t - 1)
+                blend(t - 1)
+            if in_range(t):
+                combine(t)
+            if in_range(t + 1):
+                difference(t + 1)
+            if in_range(t + 2):
+                regroup(t + 2)
+                quantise(t + 2)

@@ -82,8 +82,8 @@ def tile_layernormgrucell_pb_kernel(
         nc.sync.dma_start(out=c_sb[:, 0, :], in_=c_rows[:, 0, :])
         for t in range(1, TILES):
             nc.sync.dma_start(out=h_sb[:, t, :], in_=h_rows[:, t, :])
-            nc.sync.dma_start(out=x_sb[:, t, :], in_=x_rows[:, t, :])
             nc.sync.dma_start(out=c_sb[:, t, :], in_=c_rows[:, t, :])
+            nc.sync.dma_start(out=x_sb[:, t, :], in_=x_rows[:, t, :])
 
         identity = keep.tile([P, P], F32)
         make_identity(nc, identity[:])
@@ -103,6 +103,7 @@ def tile_layernormgrucell_pb_kernel(
         grouped = {}
         quantised = {}
         product = {}
+        mean_parts = {}
         neg_mean = {}
         sum_sq = {}
         rstd = {}
@@ -111,11 +112,9 @@ def tile_layernormgrucell_pb_kernel(
         gate = {}
 
         def difference(t):
-            for half in range(HALVES):
-                cols = slice(BANK * half, BANK * (half + 1))
-                nc.gpsimd.tensor_tensor(
-                    out=diff[:, t, cols], in0=c_sb[:, t, cols], in1=h_sb[:, t, cols], op=ALU.subtract
-                )
+            nc.vector.tensor_tensor(
+                out=diff[:, t, :], in0=c_sb[:, t, :], in1=h_sb[:, t, :], op=ALU.subtract
+            )
 
         def transpose(t):
             for j in range(2):
@@ -184,15 +183,18 @@ def tile_layernormgrucell_pb_kernel(
                         scale=-1.0 / N,
                         accum_out=parts[:, j, half : half + 1],
                     )
+            mean_parts[t] = parts
+            neg_mean[t] = minus
+
+        def join_means(t):
             for j in range(2):
                 nc.scalar.activation(
-                    out=minus[:, j : j + 1],
-                    in_=parts[:, j, 0:1],
+                    out=neg_mean[t][:, j : j + 1],
+                    in_=mean_parts[t][:, j, 0:1],
                     func=ACT.Identity,
-                    bias=parts[:, j, 1:2],
+                    bias=mean_parts[t][:, j, 1:2],
                     scale=1.0,
                 )
-            neg_mean[t] = minus
             squares = small.tile([P, 2, HALVES], F32)
             sum_sq[t] = squares
 
@@ -222,7 +224,7 @@ def tile_layernormgrucell_pb_kernel(
 
         def centre(t):
             for j in range(2):
-                scaled = work.tile([P, N], F32, bufs=4)
+                scaled = work.tile([P, N], F32, bufs=6)
                 for half in range(HALVES):
                     cols = slice(BANK * half, BANK * (half + 1))
                     nc.vector.scalar_tensor_tensor(
@@ -247,12 +249,12 @@ def tile_layernormgrucell_pb_kernel(
             )
             pre_gate[t] = total
 
-        def sigmoid(t):
-            update = work.tile([P, N], F32)
-            for half in range(HALVES):
-                cols = slice(BANK * half, BANK * (half + 1))
-                nc.scalar.activation(out=update[:, cols], in_=pre_gate[t][:, cols], func=ACT.Sigmoid)
-            gate[t] = update
+        def sigmoid(t, half):
+            if half == 0:
+                update = work.tile([P, N], F32)
+                gate[t] = update
+            cols = slice(BANK * half, BANK * (half + 1))
+            nc.scalar.activation(out=gate[t][:, cols], in_=pre_gate[t][:, cols], func=ACT.Sigmoid)
 
         def blend(t):
             result = work.tile([P, N], F32)
@@ -269,24 +271,29 @@ def tile_layernormgrucell_pb_kernel(
         def in_range(t):
             return 0 <= t < TILES
 
-        for t in range(-2, TILES + 1):
+        for t in range(-2, TILES + 2):
             if in_range(t + 2):
                 transpose(t + 2)
             if in_range(t + 1):
                 project(t + 1)
             if in_range(t):
                 means(t)
+            if in_range(t - 2):
+                sigmoid(t - 2, 0)
+            if in_range(t):
+                join_means(t)
+            if in_range(t - 2):
+                sigmoid(t - 2, 1)
+            if in_range(t):
                 squared_deviations(t, 0)
                 squared_deviations(t, 1)
                 reciprocal_deviation(t)
                 centre(t)
             if in_range(t - 1):
-                sigmoid(t - 1)
-                blend(t - 1)
-            if in_range(t):
-                combine(t)
-            if in_range(t + 1):
-                difference(t + 1)
+                combine(t - 1)
+            if in_range(t - 2):
+                blend(t - 2)
             if in_range(t + 2):
+                difference(t + 2)
                 regroup(t + 2)
                 quantise(t + 2)

@@ -22,8 +22,13 @@ GROUP_WORDS = P * PACK // 2
 BANK = 512
 HALVES = N // BANK
 EPS = 1e-5
+AHEAD = 3
 
 FLOPS = 2 * 2 * ROWS * K * N
+
+
+def half_columns(half):
+    return slice(BANK * half, BANK * (half + 1))
 
 
 def tile_layernormgrucell_pb_kernel(
@@ -47,6 +52,9 @@ def tile_layernormgrucell_pb_kernel(
         h_sb = keep.tile([P, TILES, K], BF16)
         c_sb = keep.tile([P, TILES, N], BF16)
 
+        def load(tile_sb, rows, t):
+            nc.sync.dma_start(out=tile_sb[:, t, :], in_=rows[:, t, :])
+
         def load_weight(words, scales, words_sb, planes):
             nc.vector.memset(planes[:].rearrange("p g n -> p (g n)").bitcast(I32), 0)
             for quadrant in range(4):
@@ -64,26 +72,25 @@ def tile_layernormgrucell_pb_kernel(
         w_planes = keep.tile([P, GROUPS, N], U8, align_bytes=64)
         u_words = keep.tile([P, GROUPS, 2 * N], U8, align_bytes=64)
         u_planes = keep.tile([P, GROUPS, N], U8, align_bytes=64)
-        gamma_all = keep.tile([P, 2, N], BF16)
-        beta_all = keep.tile([P, 2, N], BF16)
 
-        nc.sync.dma_start(out=h_sb[:, 0, :], in_=h_rows[:, 0, :])
-        nc.sync.dma_start(out=x_sb[:, 0, :], in_=x_rows[:, 0, :])
+        vector_rows = keep.tile([P, 3, N], BF16)
+        nc.vector.memset(vector_rows[:].rearrange("p i n -> p (i n)").bitcast(I32), 0)
+        ones = keep.tile([P, P], BF16)
+        nc.vector.memset(ones[:], 1.0)
+
+        nc.sync.dma_start(out=vector_rows[0:1, 0:2, :], in_=ln_gamma.unsqueeze(0))
+        nc.sync.dma_start(out=vector_rows[0:2, 2, :], in_=ln_beta)
+        for t in range(2):
+            load(h_sb, h_rows, t)
+            load(x_sb, x_rows, t)
         load_weight(W_u_words, W_u_scales, w_words, w_planes)
         load_weight(U_u_words, U_u_scales, u_words, u_planes)
-        nc.sync.dma_start(
-            out=gamma_all[:].rearrange("p j n -> p (j n)"),
-            in_=ln_gamma.rearrange("j n -> (j n)").partition_broadcast(P),
-        )
-        nc.sync.dma_start(
-            out=beta_all[:].rearrange("p j n -> p (j n)"),
-            in_=ln_beta.rearrange("j n -> (j n)").partition_broadcast(P),
-        )
-        nc.sync.dma_start(out=c_sb[:, 0, :], in_=c_rows[:, 0, :])
-        for t in range(1, TILES):
-            nc.sync.dma_start(out=h_sb[:, t, :], in_=h_rows[:, t, :])
-            nc.sync.dma_start(out=c_sb[:, t, :], in_=c_rows[:, t, :])
-            nc.sync.dma_start(out=x_sb[:, t, :], in_=x_rows[:, t, :])
+        for t in range(2):
+            load(c_sb, c_rows, t)
+        for t in range(2, TILES):
+            load(h_sb, h_rows, t)
+            load(c_sb, c_rows, t)
+            load(x_sb, x_rows, t)
 
         identity = keep.tile([P, P], F32)
         make_identity(nc, identity[:])
@@ -91,10 +98,10 @@ def tile_layernormgrucell_pb_kernel(
         nc.gpsimd.memset(minus_half[:], -0.5)
         first_table = keep.tile([P, 1], F32)
         nc.scalar.activation(out=first_table[:], in_=minus_half[:, 0:1], func=ACT.Sigmoid)
-        beta_sum = keep.tile([P, N], F32)
-        nc.gpsimd.tensor_tensor(
-            out=beta_sum[:], in0=beta_all[:, 0, :], in1=beta_all[:, 1, :], op=ALU.add
-        )
+
+        spread = keep.tile([P, 3, N], F32)
+        gamma = (spread[:, 0, :], spread[:, 1, :])
+        beta_sum = spread[:, 2, :]
         diff = keep.tile([P, TILES, N], F32)
 
         activations = (h_sb, x_sb)
@@ -103,13 +110,25 @@ def tile_layernormgrucell_pb_kernel(
         grouped = {}
         quantised = {}
         product = {}
-        mean_parts = {}
         neg_mean = {}
         sum_sq = {}
         rstd = {}
         centred = {}
         pre_gate = {}
         gate = {}
+
+        def spread_vectors():
+            for i in range(3):
+                for half in range(HALVES):
+                    cols = half_columns(half)
+                    bank = product_banks.tile([P, BANK], F32)
+                    nc.tensor.matmul(
+                        out=bank[:], lhsT=ones[:], rhs=vector_rows[:, i, cols], start=True, stop=True
+                    )
+                    if half == 0:
+                        nc.scalar.copy(out=spread[:, i, cols], in_=bank[:])
+                    else:
+                        nc.vector.tensor_copy(out=spread[:, i, cols], in_=bank[:])
 
         def difference(t):
             nc.vector.tensor_tensor(
@@ -164,51 +183,59 @@ def tile_layernormgrucell_pb_kernel(
                             lhsT=codes[:, g, :].bitcast(FP8X4),
                             lhsT_scale=plane[:, g, :],
                             rhs=words_sb[:, g, 2 * BANK * half : 2 * BANK * (half + 1)].bitcast(FP4X4),
-                            rhs_scale=planes[:, g, BANK * half : BANK * (half + 1)],
+                            rhs_scale=planes[:, g, half_columns(half)],
                             start=(g == 0),
                             stop=(g == GROUPS - 1),
                         )
                     product[t, j, half] = bank
 
-        def means(t):
-            parts = small.tile([P, 2, HALVES], F32)
+        def statistics(t):
+            mean_parts = small.tile([P, 2, HALVES], F32)
             minus = small.tile([P, 2], F32)
-            for j in range(2):
-                for half in range(HALVES):
-                    unused = work.tile([P, BANK], BF16)
-                    nc.scalar.activation(
-                        out=unused[:],
-                        in_=product[t, j, half][:],
-                        func=ACT.Identity,
-                        scale=-1.0 / N,
-                        accum_out=parts[:, j, half : half + 1],
-                    )
-            mean_parts[t] = parts
-            neg_mean[t] = minus
+            squares = small.tile([P, 2, HALVES], F32)
 
-        def join_means(t):
-            for j in range(2):
+            def part_of_mean(j, half):
+                unused = work.tile([P, BANK], BF16)
                 nc.scalar.activation(
-                    out=neg_mean[t][:, j : j + 1],
-                    in_=mean_parts[t][:, j, 0:1],
+                    out=unused[:],
+                    in_=product[t, j, half][:],
                     func=ACT.Identity,
-                    bias=mean_parts[t][:, j, 1:2],
+                    scale=-1.0 / N,
+                    accum_out=mean_parts[:, j, half : half + 1],
+                )
+
+            def join_mean(j):
+                nc.scalar.activation(
+                    out=minus[:, j : j + 1],
+                    in_=mean_parts[:, j, 0:1],
+                    func=ACT.Identity,
+                    bias=mean_parts[:, j, 1:2],
                     scale=1.0,
                 )
-            squares = small.tile([P, 2, HALVES], F32)
-            sum_sq[t] = squares
 
-        def squared_deviations(t, j):
-            for half in range(HALVES):
+            def part_of_squares(j, half):
                 unused = work.tile([P, BANK], BF16)
                 nc.scalar.activation(
                     out=unused[:],
                     in_=product[t, j, half][:],
                     func=ACT.Square,
-                    bias=neg_mean[t][:, j : j + 1],
+                    bias=minus[:, j : j + 1],
                     scale=1.0,
-                    accum_out=sum_sq[t][:, j, half : half + 1],
+                    accum_out=squares[:, j, half : half + 1],
                 )
+
+            part_of_mean(0, 0)
+            part_of_mean(0, 1)
+            part_of_mean(1, 0)
+            join_mean(0)
+            part_of_mean(1, 1)
+            part_of_squares(0, 0)
+            join_mean(1)
+            part_of_squares(0, 1)
+            part_of_squares(1, 0)
+            part_of_squares(1, 1)
+            neg_mean[t] = minus
+            sum_sq[t] = squares
 
         def reciprocal_deviation(t):
             variance = small.tile([P, 2], F32)
@@ -226,12 +253,12 @@ def tile_layernormgrucell_pb_kernel(
             for j in range(2):
                 scaled = work.tile([P, N], F32, bufs=6)
                 for half in range(HALVES):
-                    cols = slice(BANK * half, BANK * (half + 1))
+                    cols = half_columns(half)
                     nc.vector.scalar_tensor_tensor(
                         out=scaled[:, cols],
                         in0=product[t, j, half][:],
                         scalar=neg_mean[t][:, j : j + 1],
-                        in1=gamma_all[:, j, cols],
+                        in1=gamma[j][:, cols],
                         op0=ALU.add,
                         op1=ALU.mult,
                     )
@@ -239,30 +266,36 @@ def tile_layernormgrucell_pb_kernel(
 
         def combine(t):
             total = work.tile([P, N], F32)
-            nc.vector.scalar_tensor_tensor(
-                out=total[:], in0=centred[t, 0][:], scalar=rstd[t][:, 0:1], in1=beta_sum[:],
-                op0=ALU.mult, op1=ALU.add,
-            )
-            nc.vector.scalar_tensor_tensor(
-                out=total[:], in0=centred[t, 1][:], scalar=rstd[t][:, 1:2], in1=total[:],
-                op0=ALU.mult, op1=ALU.add,
-            )
+            for half in range(HALVES):
+                cols = half_columns(half)
+                nc.vector.scalar_tensor_tensor(
+                    out=total[:, cols], in0=centred[t, 0][:, cols], scalar=rstd[t][:, 0:1],
+                    in1=beta_sum[:, cols], op0=ALU.mult, op1=ALU.add,
+                )
+            for half in range(HALVES):
+                cols = half_columns(half)
+                nc.vector.scalar_tensor_tensor(
+                    out=total[:, cols], in0=centred[t, 1][:, cols], scalar=rstd[t][:, 1:2],
+                    in1=total[:, cols], op0=ALU.mult, op1=ALU.add,
+                )
             pre_gate[t] = total
 
-        def sigmoid(t, half):
-            if half == 0:
-                update = work.tile([P, N], F32)
-                gate[t] = update
-            cols = slice(BANK * half, BANK * (half + 1))
-            nc.scalar.activation(out=gate[t][:, cols], in_=pre_gate[t][:, cols], func=ACT.Sigmoid)
+        def sigmoid(t):
+            update = work.tile([P, N], F32)
+            for half in range(HALVES):
+                cols = half_columns(half)
+                nc.scalar.activation(out=update[:, cols], in_=pre_gate[t][:, cols], func=ACT.Sigmoid)
+            gate[t] = update
 
         def blend(t):
             result = work.tile([P, N], F32)
             for half in range(HALVES):
-                cols = slice(BANK * half, BANK * (half + 1))
+                cols = half_columns(half)
                 nc.vector.tensor_tensor(
                     out=result[:, cols], in0=gate[t][:, cols], in1=diff[:, t, cols], op=ALU.mult
                 )
+            for half in range(HALVES):
+                cols = half_columns(half)
                 nc.vector.tensor_tensor(
                     out=result[:, cols], in0=result[:, cols], in1=h_sb[:, t, cols], op=ALU.add
                 )
@@ -271,29 +304,33 @@ def tile_layernormgrucell_pb_kernel(
         def in_range(t):
             return 0 <= t < TILES
 
-        for t in range(-2, TILES + 2):
+        spread_vectors()
+        transpose(0)
+        regroup(0)
+        quantise(0)
+        transpose(1)
+        project(0)
+        regroup(1)
+        quantise(1)
+        for t in range(AHEAD):
+            difference(t)
+        for t in range(TILES + 2):
             if in_range(t + 2):
                 transpose(t + 2)
             if in_range(t + 1):
                 project(t + 1)
             if in_range(t):
-                means(t)
-            if in_range(t - 2):
-                sigmoid(t - 2, 0)
-            if in_range(t):
-                join_means(t)
-            if in_range(t - 2):
-                sigmoid(t - 2, 1)
-            if in_range(t):
-                squared_deviations(t, 0)
-                squared_deviations(t, 1)
+                statistics(t)
                 reciprocal_deviation(t)
                 centre(t)
+            if in_range(t - 2):
+                sigmoid(t - 2)
             if in_range(t - 1):
                 combine(t - 1)
             if in_range(t - 2):
                 blend(t - 2)
             if in_range(t + 2):
-                difference(t + 2)
                 regroup(t + 2)
                 quantise(t + 2)
+            if in_range(t + AHEAD):
+                difference(t + AHEAD)

@@ -131,9 +131,11 @@ def tile_layernormgrucell_pb_kernel(
                         nc.vector.tensor_copy(out=spread[:, i, cols], in_=bank[:])
 
         def difference(t):
-            nc.vector.tensor_tensor(
-                out=diff[:, t, :], in0=c_sb[:, t, :], in1=h_sb[:, t, :], op=ALU.subtract
-            )
+            for half, engine in enumerate((nc.vector, nc.gpsimd)):
+                cols = half_columns(half)
+                engine.tensor_tensor(
+                    out=diff[:, t, cols], in0=c_sb[:, t, cols], in1=h_sb[:, t, cols], op=ALU.subtract
+                )
 
         def transpose(t):
             for j in range(2):
@@ -319,16 +321,17 @@ def tile_layernormgrucell_pb_kernel(
                 transpose(t + 2)
             if in_range(t + 1):
                 project(t + 1)
+            if in_range(t - 2):
+                sigmoid(t - 2)
             if in_range(t):
                 statistics(t)
                 reciprocal_deviation(t)
-                centre(t)
-            if in_range(t - 2):
-                sigmoid(t - 2)
             if in_range(t - 1):
                 combine(t - 1)
             if in_range(t - 2):
                 blend(t - 2)
+            if in_range(t):
+                centre(t)
             if in_range(t + 2):
                 regroup(t + 2)
                 quantise(t + 2)

@@ -22,7 +22,7 @@ GROUP_WORDS = P * PACK // 2
 BANK = 512
 HALVES = N // BANK
 EPS = 1e-5
-AHEAD = 3
+AHEAD = 4
 
 FLOPS = 2 * 2 * ROWS * K * N
 
@@ -78,11 +78,12 @@ def tile_layernormgrucell_pb_kernel(
         ones = keep.tile([P, P], BF16)
         nc.vector.memset(ones[:], 1.0)
 
+        load(h_sb, h_rows, 0)
+        load(x_sb, x_rows, 0)
         nc.sync.dma_start(out=vector_rows[0:1, 0:2, :], in_=ln_gamma.unsqueeze(0))
         nc.sync.dma_start(out=vector_rows[0:2, 2, :], in_=ln_beta)
-        for t in range(2):
-            load(h_sb, h_rows, t)
-            load(x_sb, x_rows, t)
+        load(h_sb, h_rows, 1)
+        load(x_sb, x_rows, 1)
         load_weight(W_u_words, W_u_scales, w_words, w_planes)
         load_weight(U_u_words, U_u_scales, u_words, u_planes)
         for t in range(2):
@@ -131,11 +132,9 @@ def tile_layernormgrucell_pb_kernel(
                         nc.vector.tensor_copy(out=spread[:, i, cols], in_=bank[:])
 
         def difference(t):
-            for half, engine in enumerate((nc.vector, nc.gpsimd)):
-                cols = half_columns(half)
-                engine.tensor_tensor(
-                    out=diff[:, t, cols], in0=c_sb[:, t, cols], in1=h_sb[:, t, cols], op=ALU.subtract
-                )
+            nc.vector.tensor_tensor(
+                out=diff[:, t, :], in0=c_sb[:, t, :], in1=h_sb[:, t, :], op=ALU.subtract
+            )
 
         def transpose(t):
             for j in range(2):
@@ -306,10 +305,10 @@ def tile_layernormgrucell_pb_kernel(
         def in_range(t):
             return 0 <= t < TILES
 
-        spread_vectors()
         transpose(0)
         regroup(0)
         quantise(0)
+        spread_vectors()
         transpose(1)
         project(0)
         regroup(1)
@@ -321,17 +320,16 @@ def tile_layernormgrucell_pb_kernel(
                 transpose(t + 2)
             if in_range(t + 1):
                 project(t + 1)
-            if in_range(t - 2):
-                sigmoid(t - 2)
             if in_range(t):
                 statistics(t)
                 reciprocal_deviation(t)
+                centre(t)
+            if in_range(t - 2):
+                sigmoid(t - 2)
             if in_range(t - 1):
                 combine(t - 1)
             if in_range(t - 2):
                 blend(t - 2)
-            if in_range(t):
-                centre(t)
             if in_range(t + 2):
                 regroup(t + 2)
                 quantise(t + 2)

@@ -100,9 +100,8 @@ def tile_layernormgrucell_pb_kernel(
         first_table = keep.tile([P, 1], F32)
         nc.scalar.activation(out=first_table[:], in_=minus_half[:, 0:1], func=ACT.Sigmoid)
 
-        spread = keep.tile([P, 3, N], F32)
-        gamma = (spread[:, 0, :], spread[:, 1, :])
-        beta_sum = spread[:, 2, :]
+        gamma = keep.tile([P, 2, N], BF16)
+        beta_sum = keep.tile([P, N], F32)
         diff = keep.tile([P, TILES, N], F32)
 
         activations = (h_sb, x_sb)
@@ -117,19 +116,26 @@ def tile_layernormgrucell_pb_kernel(
         centred = {}
         pre_gate = {}
         gate = {}
+        result = {}
 
         def spread_vectors():
-            for i in range(3):
+            for j in range(2):
+                bank = product_banks.tile([P, N], BF16, tag="bank")
                 for half in range(HALVES):
                     cols = half_columns(half)
-                    bank = product_banks.tile([P, BANK], F32)
                     nc.tensor.matmul(
-                        out=bank[:], lhsT=ones[:], rhs=vector_rows[:, i, cols], start=True, stop=True
+                        out=bank[:, cols], lhsT=ones[:], rhs=vector_rows[:, j, cols], start=True, stop=True
                     )
-                    if half == 0:
-                        nc.scalar.copy(out=spread[:, i, cols], in_=bank[:])
-                    else:
-                        nc.vector.tensor_copy(out=spread[:, i, cols], in_=bank[:])
+                copy = nc.scalar.copy if j == 0 else nc.vector.tensor_copy
+                copy(out=gamma[:, j, :], in_=bank[:])
+            for half in range(HALVES):
+                cols = half_columns(half)
+                bank = product_banks.tile([P, BANK], F32, tag="bank")
+                nc.tensor.matmul(
+                    out=bank[:], lhsT=ones[:], rhs=vector_rows[:, 2, cols], start=True, stop=True
+                )
+                copy = nc.scalar.copy if half == 0 else nc.vector.tensor_copy
+                copy(out=beta_sum[:, cols], in_=bank[:])
 
         def difference(t):
             nc.vector.tensor_tensor(
@@ -150,34 +156,34 @@ def tile_layernormgrucell_pb_kernel(
                 turned[t, j] = bank
 
         def regroup(t):
+            lined_up = operand.tile([P, 2, GROUPS, P, PACK], BF16, align_bytes=64)
             for j in range(2):
-                lined_up = operand.tile([P, GROUPS, P, PACK], BF16, align_bytes=64)
                 nc.scalar.copy(
-                    out=lined_up[:]
+                    out=lined_up[:, j, :, :, :]
                     .rearrange("p g r t -> p (g r t)")
                     .bitcast(F32)
                     .rearrange("p (g r u) -> p g r u", g=GROUPS, u=2),
                     in_=turned[t, j][:].rearrange("p g u r -> p g r u"),
                 )
-                grouped[t, j] = lined_up
+            grouped[t] = lined_up
 
         def quantise(t):
+            codes = operand.tile([P, 2, GROUPS, P], U32, align_bytes=64)
+            plane = operand.tile([P, 2, GROUPS, P], U8, align_bytes=64)
+            nc.vector.quantize_mx(
+                out=codes[:].rearrange("p j g r -> p (j g r)").bitcast(FP8X4),
+                scales=plane[:].rearrange("p j g r -> p (j g r)"),
+                in_=grouped[t][:].rearrange("p j g r t -> p (j g r t)"),
+            )
             for j in range(2):
-                codes = operand.tile([P, GROUPS, P], U32, align_bytes=64)
-                plane = operand.tile([P, GROUPS, P], U8, align_bytes=64)
-                nc.vector.quantize_mx(
-                    out=codes[:].rearrange("p g r -> p (g r)").bitcast(FP8X4),
-                    scales=plane[:].rearrange("p g r -> p (g r)"),
-                    in_=grouped[t, j][:].rearrange("p g r t -> p (g r t)"),
-                )
-                quantised[t, j] = (codes, plane)
+                quantised[t, j] = (codes[:, j, :, :], plane[:, j, :, :])
 
         def project(t):
             for j in range(2):
                 codes, plane = quantised[t, j]
                 words_sb, planes = weights[j]
                 for half in range(HALVES):
-                    bank = product_banks.tile([P, BANK], F32)
+                    bank = product_banks.tile([P, BANK], F32, tag="bank")
                     for g in range(GROUPS):
                         nc.tensor.matmul_mx(
                             out=bank[:],
@@ -259,48 +265,51 @@ def tile_layernormgrucell_pb_kernel(
                         out=scaled[:, cols],
                         in0=product[t, j, half][:],
                         scalar=neg_mean[t][:, j : j + 1],
-                        in1=gamma[j][:, cols],
+                        in1=gamma[:, j, cols],
                         op0=ALU.add,
                         op1=ALU.mult,
                     )
                 centred[t, j] = scaled
 
-        def combine(t):
+        def pieces(t):
+            if t == TILES - 1:
+                return [half_columns(half) for half in range(HALVES)]
+            return [slice(0, N)]
+
+        def combine_first(t):
             total = work.tile([P, N], F32)
-            for half in range(HALVES):
-                cols = half_columns(half)
-                nc.vector.scalar_tensor_tensor(
-                    out=total[:, cols], in0=centred[t, 0][:, cols], scalar=rstd[t][:, 0:1],
-                    in1=beta_sum[:, cols], op0=ALU.mult, op1=ALU.add,
-                )
-            for half in range(HALVES):
-                cols = half_columns(half)
-                nc.vector.scalar_tensor_tensor(
-                    out=total[:, cols], in0=centred[t, 1][:, cols], scalar=rstd[t][:, 1:2],
-                    in1=total[:, cols], op0=ALU.mult, op1=ALU.add,
-                )
+            nc.vector.scalar_tensor_tensor(
+                out=total[:], in0=centred[t, 0][:], scalar=rstd[t][:, 0:1],
+                in1=beta_sum[:], op0=ALU.mult, op1=ALU.add,
+            )
             pre_gate[t] = total
+
+        def combine_second(t):
+            for cols in pieces(t):
+                nc.vector.scalar_tensor_tensor(
+                    out=pre_gate[t][:, cols], in0=centred[t, 1][:, cols], scalar=rstd[t][:, 1:2],
+                    in1=pre_gate[t][:, cols], op0=ALU.mult, op1=ALU.add,
+                )
 
         def sigmoid(t):
             update = work.tile([P, N], F32)
-            for half in range(HALVES):
-                cols = half_columns(half)
+            for cols in pieces(t):
                 nc.scalar.activation(out=update[:, cols], in_=pre_gate[t][:, cols], func=ACT.Sigmoid)
             gate[t] = update
 
-        def blend(t):
-            result = work.tile([P, N], F32)
-            for half in range(HALVES):
-                cols = half_columns(half)
+        def multiply(t):
+            result[t] = work.tile([P, N], F32, name="blended")
+            for cols in pieces(t):
                 nc.vector.tensor_tensor(
-                    out=result[:, cols], in0=gate[t][:, cols], in1=diff[:, t, cols], op=ALU.mult
+                    out=result[t][:, cols], in0=gate[t][:, cols], in1=diff[:, t, cols], op=ALU.mult
                 )
-            for half in range(HALVES):
-                cols = half_columns(half)
+
+        def add_h(t):
+            for cols in pieces(t):
                 nc.vector.tensor_tensor(
-                    out=result[:, cols], in0=result[:, cols], in1=h_sb[:, t, cols], op=ALU.add
+                    out=result[t][:, cols], in0=result[t][:, cols], in1=h_sb[:, t, cols], op=ALU.add
                 )
-                nc.sync.dma_start(out=out_rows[:, t, cols], in_=result[:, cols])
+                nc.sync.dma_start(out=out_rows[:, t, cols], in_=result[t][:, cols])
 
         def in_range(t):
             return 0 <= t < TILES
@@ -327,9 +336,13 @@ def tile_layernormgrucell_pb_kernel(
             if in_range(t - 2):
                 sigmoid(t - 2)
             if in_range(t - 1):
-                combine(t - 1)
+                combine_first(t - 1)
             if in_range(t - 2):
-                blend(t - 2)
+                multiply(t - 2)
+            if in_range(t - 1):
+                combine_second(t - 1)
+            if in_range(t - 2):
+                add_h(t - 2)
             if in_range(t + 2):
                 regroup(t + 2)
                 quantise(t + 2)

@@ -23,6 +23,7 @@ BANK = 512
 HALVES = N // BANK
 EPS = 1e-5
 AHEAD = 4
+TENSOR_DIFFERENCES = 5
 
 FLOPS = 2 * 2 * ROWS * K * N
 
@@ -95,6 +96,12 @@ def tile_layernormgrucell_pb_kernel(
 
         identity = keep.tile([P, P], F32)
         make_identity(nc, identity[:])
+        plus_one = keep.tile([P, P], BF16)
+        make_identity(nc, plus_one[:])
+        minus_one = keep.tile([P, P], BF16)
+        nc.gpsimd.tensor_scalar(
+            out=minus_one[:], in0=plus_one[:], scalar1=-1.0, scalar2=0.0, op0=ALU.mult, op1=ALU.add
+        )
         minus_half = keep.tile([P, 2], F32)
         nc.gpsimd.memset(minus_half[:], -0.5)
         first_table = keep.tile([P, 1], F32)
@@ -102,7 +109,8 @@ def tile_layernormgrucell_pb_kernel(
 
         gamma = keep.tile([P, 2, N], BF16)
         beta_sum = keep.tile([P, N], F32)
-        diff = keep.tile([P, TILES, N], F32)
+        early = keep.tile([P, TENSOR_DIFFERENCES, N], F32)
+        diff = {}
 
         activations = (h_sb, x_sb)
         weights = ((w_words, w_planes), (u_words, u_planes))
@@ -137,10 +145,22 @@ def tile_layernormgrucell_pb_kernel(
                 copy = nc.scalar.copy if half == 0 else nc.vector.tensor_copy
                 copy(out=beta_sum[:, cols], in_=bank[:])
 
-        def difference(t):
+        def vector_difference(t):
             nc.vector.tensor_tensor(
-                out=diff[:, t, :], in0=c_sb[:, t, :], in1=h_sb[:, t, :], op=ALU.subtract
+                out=early[:, t, :], in0=c_sb[:, t, :], in1=h_sb[:, t, :], op=ALU.subtract
             )
+
+        def tensor_difference(t):
+            for half in range(HALVES):
+                cols = half_columns(half)
+                bank = product_banks.tile([P, BANK], F32, tag="bank")
+                nc.tensor.matmul(
+                    out=bank[:], lhsT=plus_one[:], rhs=c_sb[:, t, cols], start=True, stop=False
+                )
+                nc.tensor.matmul(
+                    out=bank[:], lhsT=minus_one[:], rhs=h_sb[:, t, cols], start=False, stop=True
+                )
+                diff[t, half] = bank
 
         def transpose(t):
             for j in range(2):
@@ -299,10 +319,16 @@ def tile_layernormgrucell_pb_kernel(
 
         def multiply(t):
             result[t] = work.tile([P, N], F32, name="blended")
-            for cols in pieces(t):
+            if t < TENSOR_DIFFERENCES:
                 nc.vector.tensor_tensor(
-                    out=result[t][:, cols], in0=gate[t][:, cols], in1=diff[:, t, cols], op=ALU.mult
+                    out=result[t][:], in0=gate[t][:], in1=early[:, t, :], op=ALU.mult
                 )
+            else:
+                for half in range(HALVES):
+                    cols = half_columns(half)
+                    nc.vector.tensor_tensor(
+                        out=result[t][:, cols], in0=gate[t][:, cols], in1=diff[t, half][:], op=ALU.mult
+                    )
 
         def add_h(t):
             for cols in pieces(t):
@@ -323,7 +349,7 @@ def tile_layernormgrucell_pb_kernel(
         regroup(1)
         quantise(1)
         for t in range(AHEAD):
-            difference(t)
+            vector_difference(t)
         for t in range(TILES + 2):
             if in_range(t + 2):
                 transpose(t + 2)
@@ -346,5 +372,7 @@ def tile_layernormgrucell_pb_kernel(
             if in_range(t + 2):
                 regroup(t + 2)
                 quantise(t + 2)
-            if in_range(t + AHEAD):
-                difference(t + AHEAD)
+            if t + AHEAD < TENSOR_DIFFERENCES:
+                vector_difference(t + AHEAD)
+            if TENSOR_DIFFERENCES <= t - 1 < TILES:
+                tensor_difference(t - 1)

import concourse.mybir as mybir
from concourse.masks import make_identity

F32 = mybir.dt.float32
BF16 = mybir.dt.bfloat16
I32 = mybir.dt.int32
U32 = mybir.dt.uint32
U8 = mybir.dt.uint8
FP8X4 = mybir.dt.float8_e4m3fn_x4
FP4X4 = mybir.dt.float4_e2m1fn_x4
ACT = mybir.ActivationFunctionType
ALU = mybir.AluOpType

P = 128
ROWS = 1024
TILES = ROWS // P
K = 1024
N = 1024
PACK = 4
GROUPS = K // (P * PACK)
GROUP_WORDS = P * PACK // 2
BANK = 512
HALVES = N // BANK
EPS = 1e-5
AHEAD = 4
TENSOR_DIFFERENCES = 5

FLOPS = 2 * 2 * ROWS * K * N


def half_columns(half):
    return slice(BANK * half, BANK * (half + 1))


def tile_layernormgrucell_pb_kernel(
    tc, x, h, c, W_u_words, W_u_scales, U_u_words, U_u_scales, ln_gamma, ln_beta, out
):
    nc = tc.nc
    with (
        tc.tile_pool(name="keep", bufs=1) as keep,
        tc.tile_pool(name="operand", bufs=4) as operand,
        tc.tile_pool(name="small", bufs=4) as small,
        tc.tile_pool(name="work", bufs=3) as work,
        tc.psum_pool(name="turned_banks", bufs=2) as turned_banks,
        tc.psum_pool(name="product_banks", bufs=6) as product_banks,
        tc.manual_schedule(),
    ):
        x_rows = x.rearrange("(p t) k -> p t k", t=TILES)
        h_rows = h.rearrange("(p t) k -> p t k", t=TILES)
        c_rows = c.rearrange("(p t) k -> p t k", t=TILES)
        out_rows = out.rearrange("(p t) n -> p t n", t=TILES)
        x_sb = keep.tile([P, TILES, K], BF16)
        h_sb = keep.tile([P, TILES, K], BF16)
        c_sb = keep.tile([P, TILES, N], BF16)

        def load(tile_sb, rows, t):
            nc.sync.dma_start(out=tile_sb[:, t, :], in_=rows[:, t, :])

        def load_weight(words, scales, words_sb, planes):
            nc.vector.memset(planes[:].rearrange("p g n -> p (g n)").bitcast(I32), 0)
            for quadrant in range(4):
                nc.sync.dma_start(
                    out=planes[32 * quadrant : 32 * quadrant + 4, :, :].bitcast(I32),
                    in_=scales.bitcast(I32)[:, 4 * quadrant : 4 * quadrant + 4, :].rearrange(
                        "g r n -> r g n"
                    ),
                )
            nc.sync.dma_start(
                out=words_sb[:].bitcast(I32), in_=words.bitcast(I32).rearrange("g p b -> p g b")
            )

        w_words = keep.tile([P, GROUPS, 2 * N], U8, align_bytes=64)
        w_planes = keep.tile([P, GROUPS, N], U8, align_bytes=64)
        u_words = keep.tile([P, GROUPS, 2 * N], U8, align_bytes=64)
        u_planes = keep.tile([P, GROUPS, N], U8, align_bytes=64)

        vector_rows = keep.tile([P, 3, N], BF16)
        nc.vector.memset(vector_rows[:].rearrange("p i n -> p (i n)").bitcast(I32), 0)
        ones = keep.tile([P, P], BF16)
        nc.vector.memset(ones[:], 1.0)

        load(h_sb, h_rows, 0)
        load(x_sb, x_rows, 0)
        nc.sync.dma_start(out=vector_rows[0:1, 0:2, :], in_=ln_gamma.unsqueeze(0))
        nc.sync.dma_start(out=vector_rows[0:2, 2, :], in_=ln_beta)
        load(h_sb, h_rows, 1)
        load(x_sb, x_rows, 1)
        load_weight(W_u_words, W_u_scales, w_words, w_planes)
        load_weight(U_u_words, U_u_scales, u_words, u_planes)
        for t in range(2):
            load(c_sb, c_rows, t)
        for t in range(2, TILES):
            load(h_sb, h_rows, t)
            load(c_sb, c_rows, t)
            load(x_sb, x_rows, t)

        identity = keep.tile([P, P], F32)
        make_identity(nc, identity[:])
        plus_one = keep.tile([P, P], BF16)
        make_identity(nc, plus_one[:])
        minus_one = keep.tile([P, P], BF16)
        nc.gpsimd.tensor_scalar(
            out=minus_one[:], in0=plus_one[:], scalar1=-1.0, scalar2=0.0, op0=ALU.mult, op1=ALU.add
        )
        minus_half = keep.tile([P, 2], F32)
        nc.gpsimd.memset(minus_half[:], -0.5)
        first_table = keep.tile([P, 1], F32)
        nc.scalar.activation(out=first_table[:], in_=minus_half[:, 0:1], func=ACT.Sigmoid)

        gamma = keep.tile([P, 2, N], BF16)
        beta_sum = keep.tile([P, N], F32)
        early = keep.tile([P, TENSOR_DIFFERENCES, N], F32)
        diff = {}

        activations = (h_sb, x_sb)
        weights = ((w_words, w_planes), (u_words, u_planes))
        turned = {}
        grouped = {}
        quantised = {}
        product = {}
        neg_mean = {}
        sum_sq = {}
        rstd = {}
        centred = {}
        pre_gate = {}
        gate = {}
        result = {}

        def spread_vectors():
            for j in range(2):
                bank = product_banks.tile([P, N], BF16, tag="bank")
                for half in range(HALVES):
                    cols = half_columns(half)
                    nc.tensor.matmul(
                        out=bank[:, cols], lhsT=ones[:], rhs=vector_rows[:, j, cols], start=True, stop=True
                    )
                copy = nc.scalar.copy if j == 0 else nc.vector.tensor_copy
                copy(out=gamma[:, j, :], in_=bank[:])
            for half in range(HALVES):
                cols = half_columns(half)
                bank = product_banks.tile([P, BANK], F32, tag="bank")
                nc.tensor.matmul(
                    out=bank[:], lhsT=ones[:], rhs=vector_rows[:, 2, cols], start=True, stop=True
                )
                copy = nc.scalar.copy if half == 0 else nc.vector.tensor_copy
                copy(out=beta_sum[:, cols], in_=bank[:])

        def vector_difference(t):
            nc.vector.tensor_tensor(
                out=early[:, t, :], in0=c_sb[:, t, :], in1=h_sb[:, t, :], op=ALU.subtract
            )

        def tensor_difference(t):
            for half in range(HALVES):
                cols = half_columns(half)
                bank = product_banks.tile([P, BANK], F32, tag="bank")
                nc.tensor.matmul(
                    out=bank[:], lhsT=plus_one[:], rhs=c_sb[:, t, cols], start=True, stop=False
                )
                nc.tensor.matmul(
                    out=bank[:], lhsT=minus_one[:], rhs=h_sb[:, t, cols], start=False, stop=True
                )
                diff[t, half] = bank

        def transpose(t):
            for j in range(2):
                words = activations[j][:, t, :].bitcast(F32)
                bank = turned_banks.tile([P, GROUPS, 2, P], F32)
                for g in range(GROUPS):
                    for u in range(2):
                        nc.tensor.transpose(
                            bank[:, g, u, :],
                            words[:, GROUP_WORDS * g + u : GROUP_WORDS * (g + 1) : 2],
                            identity[:],
                        )
                turned[t, j] = bank

        def regroup(t):
            lined_up = operand.tile([P, 2, GROUPS, P, PACK], BF16, align_bytes=64)
            for j in range(2):
                nc.scalar.copy(
                    out=lined_up[:, j, :, :, :]
                    .rearrange("p g r t -> p (g r t)")
                    .bitcast(F32)
                    .rearrange("p (g r u) -> p g r u", g=GROUPS, u=2),
                    in_=turned[t, j][:].rearrange("p g u r -> p g r u"),
                )
            grouped[t] = lined_up

        def quantise(t):
            codes = operand.tile([P, 2, GROUPS, P], U32, align_bytes=64)
            plane = operand.tile([P, 2, GROUPS, P], U8, align_bytes=64)
            nc.vector.quantize_mx(
                out=codes[:].rearrange("p j g r -> p (j g r)").bitcast(FP8X4),
                scales=plane[:].rearrange("p j g r -> p (j g r)"),
                in_=grouped[t][:].rearrange("p j g r t -> p (j g r t)"),
            )
            for j in range(2):
                quantised[t, j] = (codes[:, j, :, :], plane[:, j, :, :])

        def project(t):
            for j in range(2):
                codes, plane = quantised[t, j]
                words_sb, planes = weights[j]
                for half in range(HALVES):
                    bank = product_banks.tile([P, BANK], F32, tag="bank")
                    for g in range(GROUPS):
                        nc.tensor.matmul_mx(
                            out=bank[:],
                            lhsT=codes[:, g, :].bitcast(FP8X4),
                            lhsT_scale=plane[:, g, :],
                            rhs=words_sb[:, g, 2 * BANK * half : 2 * BANK * (half + 1)].bitcast(FP4X4),
                            rhs_scale=planes[:, g, half_columns(half)],
                            start=(g == 0),
                            stop=(g == GROUPS - 1),
                        )
                    product[t, j, half] = bank

        def statistics(t):
            mean_parts = small.tile([P, 2, HALVES], F32)
            minus = small.tile([P, 2], F32)
            squares = small.tile([P, 2, HALVES], F32)

            def part_of_mean(j, half):
                unused = work.tile([P, BANK], BF16)
                nc.scalar.activation(
                    out=unused[:],
                    in_=product[t, j, half][:],
                    func=ACT.Identity,
                    scale=-1.0 / N,
                    accum_out=mean_parts[:, j, half : half + 1],
                )

            def join_mean(j):
                nc.scalar.activation(
                    out=minus[:, j : j + 1],
                    in_=mean_parts[:, j, 0:1],
                    func=ACT.Identity,
                    bias=mean_parts[:, j, 1:2],
                    scale=1.0,
                )

            def part_of_squares(j, half):
                unused = work.tile([P, BANK], BF16)
                nc.scalar.activation(
                    out=unused[:],
                    in_=product[t, j, half][:],
                    func=ACT.Square,
                    bias=minus[:, j : j + 1],
                    scale=1.0,
                    accum_out=squares[:, j, half : half + 1],
                )

            part_of_mean(0, 0)
            part_of_mean(0, 1)
            part_of_mean(1, 0)
            join_mean(0)
            part_of_mean(1, 1)
            part_of_squares(0, 0)
            join_mean(1)
            part_of_squares(0, 1)
            part_of_squares(1, 0)
            part_of_squares(1, 1)
            neg_mean[t] = minus
            sum_sq[t] = squares

        def reciprocal_deviation(t):
            variance = small.tile([P, 2], F32)
            inverse = small.tile([P, 2], F32)
            nc.gpsimd.tensor_tensor(
                out=variance[:], in0=sum_sq[t][:, :, 0], in1=sum_sq[t][:, :, 1], op=ALU.add
            )
            nc.gpsimd.tensor_scalar(
                out=variance[:], in0=variance[:], scalar1=1.0 / N, scalar2=EPS, op0=ALU.mult, op1=ALU.add
            )
            nc.gpsimd.tensor_tensor(out=inverse[:], in0=variance[:], in1=minus_half[:], op=ALU.pow)
            rstd[t] = inverse

        def centre(t):
            for j in range(2):
                scaled = work.tile([P, N], F32, bufs=6)
                for half in range(HALVES):
                    cols = half_columns(half)
                    nc.vector.scalar_tensor_tensor(
                        out=scaled[:, cols],
                        in0=product[t, j, half][:],
                        scalar=neg_mean[t][:, j : j + 1],
                        in1=gamma[:, j, cols],
                        op0=ALU.add,
                        op1=ALU.mult,
                    )
                centred[t, j] = scaled

        def pieces(t):
            if t == TILES - 1:
                return [half_columns(half) for half in range(HALVES)]
            return [slice(0, N)]

        def combine_first(t):
            total = work.tile([P, N], F32)
            nc.vector.scalar_tensor_tensor(
                out=total[:], in0=centred[t, 0][:], scalar=rstd[t][:, 0:1],
                in1=beta_sum[:], op0=ALU.mult, op1=ALU.add,
            )
            pre_gate[t] = total

        def combine_second(t):
            for cols in pieces(t):
                nc.vector.scalar_tensor_tensor(
                    out=pre_gate[t][:, cols], in0=centred[t, 1][:, cols], scalar=rstd[t][:, 1:2],
                    in1=pre_gate[t][:, cols], op0=ALU.mult, op1=ALU.add,
                )

        def sigmoid(t):
            update = work.tile([P, N], F32)
            for cols in pieces(t):
                nc.scalar.activation(out=update[:, cols], in_=pre_gate[t][:, cols], func=ACT.Sigmoid)
            gate[t] = update

        def multiply(t):
            result[t] = work.tile([P, N], F32, name="blended")
            if t < TENSOR_DIFFERENCES:
                nc.vector.tensor_tensor(
                    out=result[t][:], in0=gate[t][:], in1=early[:, t, :], op=ALU.mult
                )
            else:
                for half in range(HALVES):
                    cols = half_columns(half)
                    nc.vector.tensor_tensor(
                        out=result[t][:, cols], in0=gate[t][:, cols], in1=diff[t, half][:], op=ALU.mult
                    )

        def add_h(t):
            for cols in pieces(t):
                nc.vector.tensor_tensor(
                    out=result[t][:, cols], in0=result[t][:, cols], in1=h_sb[:, t, cols], op=ALU.add
                )
                nc.sync.dma_start(out=out_rows[:, t, cols], in_=result[t][:, cols])

        def in_range(t):
            return 0 <= t < TILES

        transpose(0)
        regroup(0)
        quantise(0)
        spread_vectors()
        transpose(1)
        project(0)
        regroup(1)
        quantise(1)
        for t in range(AHEAD):
            vector_difference(t)
        for t in range(TILES + 2):
            if in_range(t + 2):
                transpose(t + 2)
            if in_range(t + 1):
                project(t + 1)
            if in_range(t):
                statistics(t)
                reciprocal_deviation(t)
                centre(t)
            if in_range(t - 2):
                sigmoid(t - 2)
            if in_range(t - 1):
                combine_first(t - 1)
            if in_range(t - 2):
                multiply(t - 2)
            if in_range(t - 1):
                combine_second(t - 1)
            if in_range(t - 2):
                add_h(t - 2)
            if in_range(t + 2):
                regroup(t + 2)
                quantise(t + 2)
            if t + AHEAD < TENSOR_DIFFERENCES:
                vector_difference(t + AHEAD)
            if TENSOR_DIFFERENCES <= t - 1 < TILES:
                tensor_difference(t - 1)
